import numpy as np
import ml_dtypes


def mxq(x, axis, fmt="e4m3"):
    dtype, down = {"e4m3": (ml_dtypes.float8_e4m3fn, 7), "e5m2": (ml_dtypes.float8_e5m2, 14)}[fmt]
    v = np.moveaxis(np.asarray(x, np.float32).astype(ml_dtypes.bfloat16).astype(np.float64), axis, -1)
    blocks = v.reshape(v.shape[:-1] + (-1, 32))
    amax = np.abs(blocks).max(-1, keepdims=True)
    byte = np.maximum(np.where(amax > 0, np.frexp(amax)[1] - 1 + 127, 0) - down, 1)
    scale = np.exp2(byte - 127.0)
    codes = (blocks / scale).astype(np.float32).astype(dtype).astype(np.float64)
    return np.moveaxis((codes * scale).reshape(v.shape), -1, axis)


WIDE = False


def mx_kscale(k):
    if not WIDE:
        return np.ones(k)
    levels = np.array([10, -10, 5, -5, 0])
    if k % 512:
        return np.exp2(np.random.permutation(np.resize(levels, k // 32))).repeat(32)
    a = np.empty((k // 512, 16))
    for p in range(k // 512):
        a[p, :8] = np.random.permutation(np.resize(levels, 8))
        for g in range(8):
            far = levels[np.abs(levels - a[p, g]) >= 10]
            a[p, g + 8] = far[np.random.randint(len(far))]
    return np.exp2(a.ravel()).repeat(32)


BF16 = ml_dtypes.bfloat16


def bf(x):
    return np.asarray(x, np.float32).astype(BF16)


def f64(x):
    return np.asarray(x).astype(np.float64)


B, T, C, QLR, H, R, KVL, VD = 4, 1024, 1024, 1536, 4, 128, 512, 128
THETA = 10000.0
EPS = 1e-6
HALF = R // 2


def rms_norm(v, w):
    return v / np.sqrt(np.mean(v * v, axis=-1, keepdims=True) + EPS) * w


def rope_cos_sin():
    inv = 1.0 / THETA ** (np.arange(HALF) / HALF)
    ang = np.arange(T)[:, None] * inv
    return np.cos(ang), np.sin(ang)


def apply_rot(v, cos, sin):
    vr, vi = v[..., 0::2], v[..., 1::2]
    c = cos[None, :, None, :]
    s = sin[None, :, None, :]
    return np.stack([vr * c - vi * s, vr * s + vi * c], axis=-1).reshape(v.shape)


def draw0():
    s, t = mx_kscale(C), mx_kscale(KVL)
    return {"x": bf(np.random.standard_normal((B, T, C)) * s),
            "w_kva": bf(np.random.standard_normal((KVL + R, C)) / np.sqrt(C) / s),
            "kva_norm_w": bf((1.0 + 0.1 * np.random.standard_normal(KVL)) * t),
            "w_kvb": bf(np.random.standard_normal((H * (R + VD), KVL)) / np.sqrt(KVL) / t)}


def core(x, w_kva, kva_norm_w, w_kvb):
    kv_a = mxq(f64(x), 2, "e4m3") @ mxq(f64(w_kva), 1, "e4m3").T
    kv_c = rms_norm(kv_a[..., :KVL], f64(kva_norm_w))
    k_rope_raw = kv_a[..., KVL:]
    kv = (mxq(kv_c, 2, "e4m3") @ mxq(f64(w_kvb), 1, "e4m3").T).reshape(B, T, H, R + VD)
    k_content, v = kv[..., :R], kv[..., R:]
    k_rope = np.broadcast_to(k_rope_raw[:, :, None, :], (B, T, H, R))
    cos, sin = rope_cos_sin()
    k = np.concatenate([k_content, apply_rot(k_rope, cos, sin)], axis=-1)
    return k, v


def e4m3fn_bytes(y):
    return np.clip(np.asarray(y, np.float64), -448.0, 448.0).astype(np.float32).astype(ml_dtypes.float8_e4m3fn).view(np.uint8)


def e4m3fn_values(b):
    return np.asarray(b, np.uint8).view(ml_dtypes.float8_e4m3fn).astype(np.float64)


def setup_inputs():
    d = draw0()
    x0 = np.asarray(d['x']).astype(np.float64)
    s = (np.max(np.abs(x0), axis=(0, 1), keepdims=True) / 448.0).astype(np.float32)
    out = {}
    for k, v in d.items():
        if k == 'x':
            out['x_bytes'] = e4m3fn_bytes(x0 / s.astype(np.float64))
            out['x_scale'] = s
        else:
            out[k] = v
    return out


def reference(x_bytes, x_scale, w_kva, kva_norm_w, w_kvb):
    return core(e4m3fn_values(x_bytes) * x_scale.astype(np.float64), w_kva, kva_norm_w, w_kvb)

@@ -1,0 +1,321 @@
+import math
+from contextlib import ExitStack
+
+import concourse.mybir as mybir
+from concourse.masks import make_identity
+
+B, T, C, H, R, KVL, VD = 4, 1024, 1024, 4, 128, 512, 128
+THETA = 10000.0
+EPS = 1e-6
+FLOPS = 2 * B * T * C * (KVL + R) + 2 * B * T * KVL * H * (R + VD)
+
+F32 = mybir.dt.float32
+BF16 = mybir.dt.bfloat16
+I32 = mybir.dt.int32
+U32 = mybir.dt.uint32
+U8 = mybir.dt.uint8
+FP8 = mybir.dt.float8_e4m3fn
+FP8X4 = mybir.dt.float8_e4m3fn_x4
+ALU = mybir.AluOpType
+ACT = mybir.ActivationFunctionType
+
+P = 128
+ROWS = 4
+GROUPS = B * T // (P * ROWS)
+TILES = GROUPS * ROWS
+POS_TILES = T // P
+HALF = R // 2
+
+
+def tile_multiheadlatentattention_pb_t_kernel(tc, x_bytes, x_scale, w_kva, kva_norm_w, w_kvb, out_0, out_1):
+    nc = tc.nc
+    with ExitStack() as ctx:
+        sb = ctx.enter_context(tc.tile_pool(name="sb", bufs=1))
+        ps = ctx.enter_context(tc.psum_pool(name="ps", bufs=1))
+        ctx.enter_context(tc.manual_schedule())
+
+        def ring(name, count, shape, dtype):
+            return [sb.tile(shape, dtype, name="%s%d" % (name, n), align_bytes=64) for n in range(count)]
+
+        def bank(name):
+            return ps.tile([P, 512], F32, name=name)
+
+        xt_ps = [bank("xt0"), bank("xt1")]
+        l_ps = [bank("l0"), bank("l1")]
+        r_ps = bank("rp")
+        ct_ps = bank("ct")
+        k_ps = bank("kp")
+        v_ps = bank("vp")
+
+        wl_raw = ring("wl_raw", 2, [P, 4, 512], BF16)
+        wr_raw = ring("wr_raw", 1, [P, C], BF16)[0]
+        wb_raw = ring("wb_raw", 2, [P, H, KVL], BF16)
+        scale = ring("scale", 1, [P, C], F32)[0]
+        gain_raw = ring("gain_raw", 1, [P, KVL], BF16)[0]
+        xbytes = ring("xbytes", GROUPS, [P, ROWS * C], U8)
+        wl_hbm = w_kva[0:KVL, :].rearrange("(m t) k -> m t k", t=4)
+        wb_hbm = w_kvb.rearrange("(h f d) k -> f d h k", f=2, d=P)
+        x_hbm = x_bytes.rearrange("b (s p j) k -> (b s) p (j k)", p=P, j=ROWS)
+        k_hbm = out_0.rearrange("b (s p j) h d -> (b s) j p h d", p=P, j=ROWS)
+        v_hbm = out_1.rearrange("b (s p j) h d -> (b s) j p (h d)", p=P, j=ROWS)
+
+        nc.sync.dma_start(out=scale[:], in_=x_scale.rearrange("a o k -> (a o k)").partition_broadcast(P))
+        nc.sync.dma_start(out=xbytes[0][:], in_=x_hbm[0])
+        for g in range(2):
+            nc.sync.dma_start(out=wl_raw[g][:], in_=wl_hbm[:, :, 512 * g : 512 * (g + 1)])
+        nc.sync.dma_start(out=wr_raw[:], in_=w_kva[KVL : KVL + R, :])
+        nc.sync.dma_start(out=gain_raw[:], in_=kva_norm_w.partition_broadcast(P))
+        for f in range(2):
+            nc.sync.dma_start(out=wb_raw[f][:], in_=wb_hbm[f])
+        for n in range(1, GROUPS):
+            nc.sync.dma_start(out=xbytes[n][:], in_=x_hbm[n])
+
+        pos = ring("pos", 1, [P, POS_TILES], I32)[0]
+        nc.gpsimd.iota(pos[:], pattern=[[P * ROWS, POS_TILES // ROWS], [1, ROWS]], base=0, channel_multiplier=ROWS)
+        ident = ring("ident", 1, [P, P], F32)[0]
+        make_identity(nc, ident[:])
+
+        fine = ring("fine", 1, [P, 8], F32)[0]
+        one = ring("one", 1, [P, 1], F32)[0]
+        coarse = ring("coarse", 1, [P, 8, POS_TILES], F32)[0]
+        turns = ring("turns", 1, [P, POS_TILES, 8, 8], F32)[0]
+        whole = ring("whole", 1, [P, POS_TILES * HALF], I32)[0]
+        frac = ring("frac", 1, [P, POS_TILES * HALF], F32)[0]
+        mag = ring("mag", 1, [P, POS_TILES * HALF], F32)[0]
+        planes = ring("planes", 1, [P, 3, POS_TILES * HALF], F32)[0]
+        table = ring("table", 1, [P, POS_TILES // 2, 2, R, 2], F32)[0]
+        nc.vector.memset(one[:], 1.0)
+        for q in range(8):
+            nc.vector.tensor_scalar(out=coarse[:, q, :], in0=pos[:], scalar1=THETA ** (-8 * q / HALF) / (2 * math.pi), scalar2=None, op0=ALU.mult)
+        for q in range(8):
+            nc.vector.tensor_scalar(out=fine[:, q : q + 1], in0=one[:], scalar1=THETA ** (-q / HALF), scalar2=None, op0=ALU.mult)
+        nc.vector.tensor_tensor(
+            out=turns[:],
+            in0=coarse[:].rearrange("p q s -> p s q").unsqueeze(3).to_broadcast([P, POS_TILES, 8, 8]),
+            in1=fine[:].unsqueeze(1).unsqueeze(1).to_broadcast([P, POS_TILES, 8, 8]),
+            op=ALU.mult,
+        )
+        turns_flat = turns[:].rearrange("p s q r -> p (s q r)")
+        nc.vector.tensor_copy(out=whole[:], in_=turns_flat)
+        nc.vector.tensor_tensor(out=frac[:], in0=turns_flat, in1=whole[:], op=ALU.subtract)
+        nc.vector.scalar_tensor_tensor(out=mag[:], in0=frac[:], scalar=-1.0, in1=frac[:], op0=ALU.mult, op1=ALU.max)
+        nc.scalar.activation(out=planes[:, 0, :], in_=frac[:], func=ACT.Sin, scale=-2 * math.pi)
+        nc.scalar.activation(out=planes[:, 2, :], in_=frac[:], func=ACT.Sin, scale=2 * math.pi)
+        nc.scalar.activation(out=planes[:, 1, :], in_=mag[:], func=ACT.Sin, scale=-2 * math.pi, bias=math.pi / 2)
+        warm = ring("warm", 1, [P, 1], F32)[0]
+        nc.scalar.activation(out=warm[:], in_=one[:], func=ACT.Abs_reciprocal_sqrt)
+
+        def build_table():
+            for a in range(2):
+                nc.vector.tensor_copy(
+                    out=table[:, :, a, :, :],
+                    in_=planes[:, 1 - a : 3 - a, :].rearrange("p b (s j) -> p s j b", j=R),
+                )
+
+        gain = ring("gain", 1, [P, KVL], F32)[0]
+
+        def build_gain():
+            nc.vector.tensor_copy(
+                out=gain[:].rearrange("p (u m e) -> p u m e", u=2, e=2),
+                in_=gain_raw[:].rearrange("p (m u e) -> p u m e", u=2, e=2),
+            )
+
+        wl_g = ring("wl_g", 2, [P, 2048], BF16)
+        wl_codes = ring("wl_codes", 2, [P, 512], U32)
+        wl_sc = ring("wl_sc", 2, [P, 512], U8)
+        wr_g = ring("wr_g", 1, [P, 1024], BF16)[0]
+        wr_codes = ring("wr_codes", 1, [P, 256], U32)[0]
+        wr_sc = ring("wr_sc", 1, [P, 256], U8)[0]
+        wb_g = ring("wb_g", 2, [P, 2048], BF16)
+        wb_codes = ring("wb_codes", 2, [P, 512], U32)
+        wb_sc = ring("wb_sc", 2, [P, 512], U8)
+
+        def copy_on(engine, out, in_):
+            if engine == "v":
+                nc.vector.tensor_copy(out=out, in_=in_)
+            else:
+                nc.scalar.copy(out=out, in_=in_)
+
+        def quantize(codes, sc, src):
+            nc.vector.quantize_mx(out=codes[:].bitcast(FP8X4), scales=sc[:], in_=src[:])
+
+        def turn_pass(dst, col, words, start):
+            for w in range(2):
+                nc.tensor.transpose(dst[:, col + P * w : col + P * (w + 1)], words[:, start + w : start + 256 : 2], ident[:])
+
+        def turn_wl(g, u, dst):
+            words = wl_raw[g][:].rearrange("p t k -> p (t k)").bitcast(F32)
+            for e in range(2):
+                turn_pass(dst, 256 * e, words, 256 * (2 * u + e))
+
+        def empty_wl(g, u, src, engine):
+            out = wl_g[g][:].bitcast(F32)[:, 512 * u : 512 * (u + 1)].rearrange("p (m n) -> p m n", n=4)
+            copy_on(engine, out, src[:].rearrange("p (n m) -> p m n", n=4))
+
+        def turn_rows(raw, dst):
+            words = raw.bitcast(F32)
+            for g in range(2):
+                turn_pass(dst, 256 * g, words, 256 * g)
+
+        def empty_rows(out, src, engine):
+            copy_on(engine, out.bitcast(F32).rearrange("p (g r w) -> p g r w", g=2, w=2), src[:].rearrange("p (g w r) -> p g r w", g=2, w=2))
+
+        xw = ring("xw", 4, [P, C], BF16)
+        xg = ring("xg", 2, [P, 2 * C], BF16)
+        x_codes = ring("x_codes", 2, [P, 512], U32)
+        x_sc = ring("x_sc", 2, [P, 512], U8)
+        squares = ring("squares", 2, [P, KVL], BF16)
+        ssum = ring("ssum", 3, [P, 1], F32)
+        rstd = ring("rstd", 3, [P, 1], F32)
+        cn = ring("cn", 4, [P, KVL], BF16)
+        cg = ring("cg", 2, [P, 2 * KVL], BF16)
+        c_codes = ring("c_codes", 2, [P, 2 * P], U32)
+        c_sc = ring("c_sc", 2, [P, 2 * P], U8)
+        prod = ring("prod", 2, [P, 4 * R], F32)
+        rope = ring("rope", 3, [P, 2, R], F32)
+        kout = ring("kout", 4, [P, H, R], F32)
+        vout = ring("vout", 4, [P, H * VD], F32)
+
+        def at(tiles, i):
+            return tiles[i % len(tiles)]
+
+        def widen(i):
+            src = xbytes[i // ROWS][:, C * (i % ROWS) : C * (i % ROWS + 1)]
+            nc.vector.tensor_tensor(out=at(xw, i)[:], in0=src.bitcast(FP8), in1=scale[:], op=ALU.mult)
+
+        def turn_x(i):
+            turn_rows(at(xw, i)[:], at(xt_ps, i))
+
+        def empty_x(i):
+            empty_rows(at(xg, i // 2)[:, C * (i % 2) : C * (i % 2 + 1)], at(xt_ps, i), "s")
+
+        def quant_x(n):
+            quantize(at(x_codes, n), at(x_sc, n), at(xg, n))
+
+        def mm_a(i, out, codes, sc):
+            for g in range(2):
+                cols = slice(P * (2 * (i % 2) + g), P * (2 * (i % 2) + g + 1))
+                nc.tensor.matmul_mx(
+                    out=out, lhsT=at(x_codes, i // 2)[:, cols].bitcast(FP8X4), lhsT_scale=at(x_sc, i // 2)[:, cols],
+                    rhs=codes[g].bitcast(FP8X4), rhs_scale=sc[g], start=(g == 0), stop=(g == 1),
+                )
+
+        def mm_l(i):
+            mm_a(i, at(l_ps, i)[:], [t[:] for t in wl_codes], [t[:] for t in wl_sc])
+
+        def mm_r(i):
+            mm_a(i, r_ps[:, R * (i % 2) : R * (i % 2 + 1)], [wr_codes[:, 0:P], wr_codes[:, P : 2 * P]], [wr_sc[:, 0:P], wr_sc[:, P : 2 * P]])
+
+        def sum_squares(i):
+            nc.scalar.activation(out=at(squares, i)[:], in_=at(l_ps, i)[:], func=ACT.Square, accum_out=at(ssum, i)[:])
+
+        def inv_root(i):
+            nc.scalar.activation(out=at(rstd, i)[:], in_=at(ssum, i)[:], func=ACT.Abs_reciprocal_sqrt, scale=1.0 / KVL, bias=EPS)
+
+        def normalise(i):
+            nc.vector.scalar_tensor_tensor(out=at(cn, i)[:], in0=at(l_ps, i)[:], scalar=at(rstd, i)[:], in1=gain[:], op0=ALU.mult, op1=ALU.mult)
+
+        def rope_products(n):
+            nc.vector.tensor_tensor(
+                out=at(prod, n)[:].rearrange("p (a j b) -> p a j b", a=2, b=2),
+                in0=r_ps[:, 0 : 2 * R].rearrange("p (j a) -> p a j", a=2).unsqueeze(3).to_broadcast([P, 2, R, 2]),
+                in1=table[:, n % (POS_TILES // 2), :, :, :],
+                op=ALU.mult,
+            )
+
+        def rope_sum(n):
+            nc.vector.tensor_tensor(out=at(rope, n)[:].rearrange("p t d -> p (t d)"), in0=at(prod, n)[:, 0 : 2 * R], in1=at(prod, n)[:, 2 * R : 4 * R], op=ALU.add)
+            for t in range(2):
+                i = 2 * n + t
+                nc.sync.dma_start(out=k_hbm[i // ROWS, i % ROWS][:, :, R : 2 * R], in_=at(rope, n)[:, t : t + 1, :].to_broadcast([P, H, R]))
+
+        def turn_c(n):
+            for t in range(2):
+                words = at(cn, 2 * n + t)[:].bitcast(F32)
+                for u in range(2):
+                    nc.tensor.transpose(ct_ps[:, P * (2 * t + u) : P * (2 * t + u + 1)], words[:, P * u : P * (u + 1)], ident[:])
+
+        def empty_c(n):
+            empty_rows(at(cg, n)[:], ct_ps, "s")
+
+        def quant_c(n):
+            quantize(at(c_codes, n), at(c_sc, n), at(cg, n))
+
+        def mm_b(i):
+            cols = slice(P * (i % 2), P * (i % 2 + 1))
+            for f, out in enumerate((k_ps, v_ps)):
+                nc.tensor.matmul_mx(
+                    out=out[:], lhsT=at(c_codes, i // 2)[:, cols].bitcast(FP8X4), lhsT_scale=at(c_sc, i // 2)[:, cols],
+                    rhs=wb_codes[f][:].bitcast(FP8X4), rhs_scale=wb_sc[f][:], start=True, stop=True,
+                )
+
+        def finish_k(i):
+            nc.scalar.copy(out=at(kout, i)[:].rearrange("p h d -> p (h d)"), in_=k_ps[:])
+
+        def store_k(i):
+            nc.sync.dma_start(out=k_hbm[i // ROWS, i % ROWS][:, :, 0:R], in_=at(kout, i)[:])
+
+        def finish_v(i):
+            nc.scalar.copy(out=at(vout, i)[:], in_=v_ps[:])
+            nc.sync.dma_start(out=v_hbm[i // ROWS, i % ROWS], in_=at(vout, i)[:])
+
+        def run(stage, i):
+            if 0 <= i < TILES:
+                stage(i)
+
+        def run_pair(stage, i):
+            if 0 <= i < TILES and i % 2 == 0:
+                stage(i // 2)
+
+        head_banks = [l_ps[0], l_ps[1], k_ps, v_ps]
+        widen(0)
+        widen(1)
+        for g in range(2):
+            for u in range(2):
+                turn_wl(g, u, head_banks[2 * g + u])
+        turn_rows(wr_raw[:], r_ps)
+        for u in range(2):
+            empty_wl(0, u, head_banks[u], "v")
+        build_gain()
+        quantize(wl_codes[0], wl_sc[0], wl_g[0])
+        for u in range(2):
+            empty_wl(1, u, head_banks[2 + u], "s")
+        empty_rows(wr_g[:], r_ps, "s")
+        build_table()
+        quantize(wl_codes[1], wl_sc[1], wl_g[1])
+        quantize(wr_codes, wr_sc, wr_g)
+
+        def prepare_wb(f):
+            flat = wb_raw[f][:].rearrange("p h k -> p (h k)")
+            for half, dst in enumerate((k_ps, v_ps)):
+                turn_rows(flat[:, 1024 * half : 1024 * (half + 1)], dst)
+
+        def empty_wb(f):
+            for half, src in enumerate((k_ps, v_ps)):
+                empty_rows(wb_g[f][:, 1024 * half : 1024 * (half + 1)], src, "s")
+
+        for s in range(TILES + 7):
+            run(finish_v, s - 7)
+            run(turn_x, s)
+            run_pair(turn_c, s - 5)
+            if s in (0, 1):
+                prepare_wb(s)
+            run(widen, s + 2)
+            run_pair(rope_products, s - 4)
+            run(normalise, s - 3)
+            run_pair(rope_sum, s - 4)
+            run(empty_x, s)
+            if s in (0, 1):
+                empty_wb(s)
+            run_pair(empty_c, s - 5)
+            run(mm_l, s - 2)
+            run(mm_b, s - 6)
+            run(mm_r, s - 2)
+            run_pair(quant_x, s - 1)
+            run_pair(quant_c, s - 5)
+            if s in (0, 1):
+                quantize(wb_codes[s], wb_sc[s], wb_g[s])
+            run(sum_squares, s - 2)
+            run(finish_k, s - 6)
+            run(inv_root, s - 2)
+            run(store_k, s - 6)

@@ -51,7 +51,8 @@ def tile_multiheadlatentattention_pb_t_kernel(tc, x_bytes, x_scale, w_kva, kva_n
         wr_raw = ring("wr_raw", 1, [P, C], BF16)[0]
         wb_raw = ring("wb_raw", 2, [P, H, KVL], BF16)
         scale = ring("scale", 1, [P, C], F32)[0]
-        gain_raw = ring("gain_raw", 1, [P, KVL], BF16)[0]
+        scale_raw = ring("scale_raw", 1, [P, C // P], F32)[0]
+        gain_raw = ring("gain_raw", 1, [P, KVL // P], BF16)[0]
         xbytes = ring("xbytes", GROUPS, [P, ROWS * C], U8)
         wl_hbm = w_kva[0:KVL, :].rearrange("(m t) k -> m t k", t=4)
         wb_hbm = w_kvb.rearrange("(h f d) k -> f d h k", f=2, d=P)
@@ -59,12 +60,12 @@ def tile_multiheadlatentattention_pb_t_kernel(tc, x_bytes, x_scale, w_kva, kva_n
         k_hbm = out_0.rearrange("b (s p j) h d -> (b s) j p h d", p=P, j=ROWS)
         v_hbm = out_1.rearrange("b (s p j) h d -> (b s) j p (h d)", p=P, j=ROWS)
 
-        nc.sync.dma_start(out=scale[:], in_=x_scale.rearrange("a o k -> (a o k)").partition_broadcast(P))
+        nc.sync.dma_start(out=scale_raw[:], in_=x_scale.rearrange("a o (p j) -> p (a o j)", p=P))
+        nc.sync.dma_start(out=gain_raw[:], in_=kva_norm_w.rearrange("(p j) -> p j", p=P))
+        nc.sync.dma_start(out=wl_raw[0][:], in_=wl_hbm[:, :, 0:512])
         nc.sync.dma_start(out=xbytes[0][:], in_=x_hbm[0])
-        for g in range(2):
-            nc.sync.dma_start(out=wl_raw[g][:], in_=wl_hbm[:, :, 512 * g : 512 * (g + 1)])
+        nc.sync.dma_start(out=wl_raw[1][:], in_=wl_hbm[:, :, 512:1024])
         nc.sync.dma_start(out=wr_raw[:], in_=w_kva[KVL : KVL + R, :])
-        nc.sync.dma_start(out=gain_raw[:], in_=kva_norm_w.partition_broadcast(P))
         for f in range(2):
             nc.sync.dma_start(out=wb_raw[f][:], in_=wb_hbm[f])
         for n in range(1, GROUPS):
@@ -83,8 +84,14 @@ def tile_multiheadlatentattention_pb_t_kernel(tc, x_bytes, x_scale, w_kva, kva_n
         frac = ring("frac", 1, [P, POS_TILES * HALF], F32)[0]
         mag = ring("mag", 1, [P, POS_TILES * HALF], F32)[0]
         planes = ring("planes", 1, [P, 3, POS_TILES * HALF], F32)[0]
-        table = ring("table", 1, [P, POS_TILES // 2, 2, R, 2], F32)[0]
+        table = ring("table", 1, [P, POS_TILES, 2, HALF, 2], F32)[0]
+        zeros = ring("zeros", 1, [P, 512], BF16)[0]
         nc.vector.memset(one[:], 1.0)
+        nc.vector.memset(zeros[:], 0.0)
+
+        def keep_clock():
+            nc.tensor.matmul(ct_ps[:], lhsT=zeros[:, 0:P], rhs=zeros[:], start=True, stop=True)
+
         for q in range(8):
             nc.vector.tensor_scalar(out=coarse[:, q, :], in0=pos[:], scalar1=THETA ** (-8 * q / HALF) / (2 * math.pi), scalar2=None, op0=ALU.mult)
         for q in range(8):
@@ -98,27 +105,30 @@ def tile_multiheadlatentattention_pb_t_kernel(tc, x_bytes, x_scale, w_kva, kva_n
         turns_flat = turns[:].rearrange("p s q r -> p (s q r)")
         nc.vector.tensor_copy(out=whole[:], in_=turns_flat)
         nc.vector.tensor_tensor(out=frac[:], in0=turns_flat, in1=whole[:], op=ALU.subtract)
-        nc.vector.scalar_tensor_tensor(out=mag[:], in0=frac[:], scalar=-1.0, in1=frac[:], op0=ALU.mult, op1=ALU.max)
-        nc.scalar.activation(out=planes[:, 0, :], in_=frac[:], func=ACT.Sin, scale=-2 * math.pi)
-        nc.scalar.activation(out=planes[:, 2, :], in_=frac[:], func=ACT.Sin, scale=2 * math.pi)
-        nc.scalar.activation(out=planes[:, 1, :], in_=mag[:], func=ACT.Sin, scale=-2 * math.pi, bias=math.pi / 2)
-        warm = ring("warm", 1, [P, 1], F32)[0]
-        nc.scalar.activation(out=warm[:], in_=one[:], func=ACT.Abs_reciprocal_sqrt)
+        warm = ring("warm", 2, [P, 1], F32)
 
-        def build_table():
-            for a in range(2):
-                nc.vector.tensor_copy(
-                    out=table[:, :, a, :, :],
-                    in_=planes[:, 1 - a : 3 - a, :].rearrange("p b (s j) -> p s j b", j=R),
-                )
+        def build_planes():
+            nc.scalar.activation(out=mag[:], in_=frac[:], func=ACT.Abs)
+            nc.scalar.activation(out=planes[:, 0, :], in_=frac[:], func=ACT.Sin, scale=-2 * math.pi)
+            nc.scalar.activation(out=planes[:, 2, :], in_=frac[:], func=ACT.Sin, scale=2 * math.pi)
+            nc.scalar.activation(out=planes[:, 1, :], in_=mag[:], func=ACT.Sin, scale=-2 * math.pi, bias=math.pi / 2)
+
+        def build_table(a, engine):
+            copy_on(engine, table[:, :, a, :, :], planes[:, 1 - a : 3 - a, :].rearrange("p b (s j) -> p s j b", j=HALF))
 
         gain = ring("gain", 1, [P, KVL], F32)[0]
 
-        def build_gain():
-            nc.vector.tensor_copy(
-                out=gain[:].rearrange("p (u m e) -> p u m e", u=2, e=2),
-                in_=gain_raw[:].rearrange("p (m u e) -> p u m e", u=2, e=2),
-            )
+        gain_wide = ring("gain_wide", 1, [P, KVL // P], F32)[0]
+
+        def spread(src, first, dst):
+            for j in range(4):
+                nc.tensor.transpose(dst[:, P * j : P * (j + 1)], src[:, first + j : first + j + 1].to_broadcast([P, P]), ident[:])
+
+        def empty_scale(half, src):
+            nc.scalar.copy(out=scale[:].rearrange("p (n j) -> p n j", j=8)[:, :, 4 * half : 4 * half + 4], in_=src[:].rearrange("p (j n) -> p n j", j=4))
+
+        def empty_gain(src):
+            nc.vector.tensor_copy(out=gain[:].rearrange("p (u m e) -> p u m e", u=2, e=2), in_=src[:].rearrange("p (u e m) -> p u m e", u=2, e=2))
 
         wl_g = ring("wl_g", 2, [P, 2048], BF16)
         wl_codes = ring("wl_codes", 2, [P, 512], U32)
@@ -161,20 +171,20 @@ def tile_multiheadlatentattention_pb_t_kernel(tc, x_bytes, x_scale, w_kva, kva_n
             copy_on(engine, out.bitcast(F32).rearrange("p (g r w) -> p g r w", g=2, w=2), src[:].rearrange("p (g w r) -> p g r w", g=2, w=2))
 
         xw = ring("xw", 4, [P, C], BF16)
-        xg = ring("xg", 2, [P, 2 * C], BF16)
-        x_codes = ring("x_codes", 2, [P, 512], U32)
-        x_sc = ring("x_sc", 2, [P, 512], U8)
+        xg = ring("xg", 2, [P, C], BF16)
+        x_codes = ring("x_codes", 3, [P, 256], U32)
+        x_sc = ring("x_sc", 3, [P, 256], U8)
         squares = ring("squares", 2, [P, KVL], BF16)
         ssum = ring("ssum", 3, [P, 1], F32)
         rstd = ring("rstd", 3, [P, 1], F32)
-        cn = ring("cn", 4, [P, KVL], BF16)
-        cg = ring("cg", 2, [P, 2 * KVL], BF16)
-        c_codes = ring("c_codes", 2, [P, 2 * P], U32)
-        c_sc = ring("c_sc", 2, [P, 2 * P], U8)
-        prod = ring("prod", 2, [P, 4 * R], F32)
-        rope = ring("rope", 3, [P, 2, R], F32)
-        kout = ring("kout", 4, [P, H, R], F32)
-        vout = ring("vout", 4, [P, H * VD], F32)
+        cn = ring("cn", 3, [P, KVL], BF16)
+        cg = ring("cg", 2, [P, KVL], BF16)
+        c_codes = ring("c_codes", 3, [P, P], U32)
+        c_sc = ring("c_sc", 3, [P, P], U8)
+        prod = ring("prod", 2, [P, 2 * R], F32)
+        rope = ring("rope", 6, [P, 1, R], F32)
+        kout = ring("kout", 6, [P, H, R], F32)
+        vout = ring("vout", 6, [P, H * VD], F32)
 
         def at(tiles, i):
             return tiles[i % len(tiles)]
@@ -187,16 +197,16 @@ def tile_multiheadlatentattention_pb_t_kernel(tc, x_bytes, x_scale, w_kva, kva_n
             turn_rows(at(xw, i)[:], at(xt_ps, i))
 
         def empty_x(i):
-            empty_rows(at(xg, i // 2)[:, C * (i % 2) : C * (i % 2 + 1)], at(xt_ps, i), "s")
+            empty_rows(at(xg, i)[:], at(xt_ps, i), "s")
 
-        def quant_x(n):
-            quantize(at(x_codes, n), at(x_sc, n), at(xg, n))
+        def quant_x(i):
+            quantize(at(x_codes, i), at(x_sc, i), at(xg, i))
 
         def mm_a(i, out, codes, sc):
             for g in range(2):
-                cols = slice(P * (2 * (i % 2) + g), P * (2 * (i % 2) + g + 1))
+                cols = slice(P * g, P * (g + 1))
                 nc.tensor.matmul_mx(
-                    out=out, lhsT=at(x_codes, i // 2)[:, cols].bitcast(FP8X4), lhsT_scale=at(x_sc, i // 2)[:, cols],
+                    out=out, lhsT=at(x_codes, i)[:, cols].bitcast(FP8X4), lhsT_scale=at(x_sc, i)[:, cols],
                     rhs=codes[g].bitcast(FP8X4), rhs_scale=sc[g], start=(g == 0), stop=(g == 1),
                 )
 
@@ -204,7 +214,7 @@ def tile_multiheadlatentattention_pb_t_kernel(tc, x_bytes, x_scale, w_kva, kva_n
             mm_a(i, at(l_ps, i)[:], [t[:] for t in wl_codes], [t[:] for t in wl_sc])
 
         def mm_r(i):
-            mm_a(i, r_ps[:, R * (i % 2) : R * (i % 2 + 1)], [wr_codes[:, 0:P], wr_codes[:, P : 2 * P]], [wr_sc[:, 0:P], wr_sc[:, P : 2 * P]])
+            mm_a(i, r_ps[:, 0:R], [wr_codes[:, 0:P], wr_codes[:, P : 2 * P]], [wr_sc[:, 0:P], wr_sc[:, P : 2 * P]])
 
         def sum_squares(i):
             nc.scalar.activation(out=at(squares, i)[:], in_=at(l_ps, i)[:], func=ACT.Square, accum_out=at(ssum, i)[:])
@@ -215,107 +225,155 @@ def tile_multiheadlatentattention_pb_t_kernel(tc, x_bytes, x_scale, w_kva, kva_n
         def normalise(i):
             nc.vector.scalar_tensor_tensor(out=at(cn, i)[:], in0=at(l_ps, i)[:], scalar=at(rstd, i)[:], in1=gain[:], op0=ALU.mult, op1=ALU.mult)
 
-        def rope_products(n):
+        def rope_products(i):
             nc.vector.tensor_tensor(
-                out=at(prod, n)[:].rearrange("p (a j b) -> p a j b", a=2, b=2),
-                in0=r_ps[:, 0 : 2 * R].rearrange("p (j a) -> p a j", a=2).unsqueeze(3).to_broadcast([P, 2, R, 2]),
-                in1=table[:, n % (POS_TILES // 2), :, :, :],
+                out=at(prod, i)[:].rearrange("p (a j b) -> p a j b", a=2, b=2),
+                in0=r_ps[:, 0:R].rearrange("p (j a) -> p a j", a=2).unsqueeze(3).to_broadcast([P, 2, HALF, 2]),
+                in1=table[:, i % POS_TILES, :, :, :],
                 op=ALU.mult,
             )
 
-        def rope_sum(n):
-            nc.vector.tensor_tensor(out=at(rope, n)[:].rearrange("p t d -> p (t d)"), in0=at(prod, n)[:, 0 : 2 * R], in1=at(prod, n)[:, 2 * R : 4 * R], op=ALU.add)
-            for t in range(2):
-                i = 2 * n + t
-                nc.sync.dma_start(out=k_hbm[i // ROWS, i % ROWS][:, :, R : 2 * R], in_=at(rope, n)[:, t : t + 1, :].to_broadcast([P, H, R]))
+        def rope_sum(i):
+            nc.vector.tensor_tensor(out=at(rope, i)[:, 0, :], in0=at(prod, i)[:, 0:R], in1=at(prod, i)[:, R : 2 * R], op=ALU.add)
+            nc.sync.dma_start(out=k_hbm[i // ROWS, i % ROWS][:, :, R : 2 * R], in_=at(rope, i)[:].to_broadcast([P, H, R]))
 
-        def turn_c(n):
-            for t in range(2):
-                words = at(cn, 2 * n + t)[:].bitcast(F32)
-                for u in range(2):
-                    nc.tensor.transpose(ct_ps[:, P * (2 * t + u) : P * (2 * t + u + 1)], words[:, P * u : P * (u + 1)], ident[:])
+        def turn_c(i):
+            words = at(cn, i)[:].bitcast(F32)
+            for u in range(2):
+                nc.tensor.transpose(ct_ps[:, P * u : P * (u + 1)], words[:, P * u : P * (u + 1)], ident[:])
 
-        def empty_c(n):
-            empty_rows(at(cg, n)[:], ct_ps, "s")
+        def empty_c(i):
+            nc.scalar.copy(out=at(cg, i)[:].bitcast(F32).rearrange("p (r u) -> p r u", u=2), in_=ct_ps[:, 0 : 2 * P].rearrange("p (u r) -> p r u", u=2))
 
-        def quant_c(n):
-            quantize(at(c_codes, n), at(c_sc, n), at(cg, n))
+        def quant_c(i):
+            quantize(at(c_codes, i), at(c_sc, i), at(cg, i))
 
-        def mm_b(i):
-            cols = slice(P * (i % 2), P * (i % 2 + 1))
-            for f, out in enumerate((k_ps, v_ps)):
-                nc.tensor.matmul_mx(
-                    out=out[:], lhsT=at(c_codes, i // 2)[:, cols].bitcast(FP8X4), lhsT_scale=at(c_sc, i // 2)[:, cols],
-                    rhs=wb_codes[f][:].bitcast(FP8X4), rhs_scale=wb_sc[f][:], start=True, stop=True,
-                )
+        def mm_b(i, f, out):
+            nc.tensor.matmul_mx(
+                out=out[:], lhsT=at(c_codes, i)[:].bitcast(FP8X4), lhsT_scale=at(c_sc, i)[:],
+                rhs=wb_codes[f][:].bitcast(FP8X4), rhs_scale=wb_sc[f][:], start=True, stop=True,
+            )
 
-        def finish_k(i):
-            nc.scalar.copy(out=at(kout, i)[:].rearrange("p h d -> p (h d)"), in_=k_ps[:])
+        def finish_k(i, src):
+            nc.scalar.copy(out=at(kout, i)[:].rearrange("p h d -> p (h d)"), in_=src[:])
 
         def store_k(i):
             nc.sync.dma_start(out=k_hbm[i // ROWS, i % ROWS][:, :, 0:R], in_=at(kout, i)[:])
 
-        def finish_v(i):
-            nc.scalar.copy(out=at(vout, i)[:], in_=v_ps[:])
+        def finish_v(i, src, engine):
+            copy_on(engine, at(vout, i)[:], src[:])
             nc.sync.dma_start(out=v_hbm[i // ROWS, i % ROWS], in_=at(vout, i)[:])
 
         def run(stage, i):
             if 0 <= i < TILES:
                 stage(i)
 
-        def run_pair(stage, i):
-            if 0 <= i < TILES and i % 2 == 0:
-                stage(i // 2)
-
-        head_banks = [l_ps[0], l_ps[1], k_ps, v_ps]
-        widen(0)
-        widen(1)
-        for g in range(2):
-            for u in range(2):
-                turn_wl(g, u, head_banks[2 * g + u])
-        turn_rows(wr_raw[:], r_ps)
-        for u in range(2):
-            empty_wl(0, u, head_banks[u], "v")
-        build_gain()
-        quantize(wl_codes[0], wl_sc[0], wl_g[0])
-        for u in range(2):
-            empty_wl(1, u, head_banks[2 + u], "s")
-        empty_rows(wr_g[:], r_ps, "s")
-        build_table()
-        quantize(wl_codes[1], wl_sc[1], wl_g[1])
-        quantize(wr_codes, wr_sc, wr_g)
-
-        def prepare_wb(f):
+        def turn_wb(n):
+            f, half = divmod(n, 2)
             flat = wb_raw[f][:].rearrange("p h k -> p (h k)")
-            for half, dst in enumerate((k_ps, v_ps)):
-                turn_rows(flat[:, 1024 * half : 1024 * (half + 1)], dst)
+            turn_rows(flat[:, 1024 * half : 1024 * (half + 1)], (k_ps, v_ps)[half])
 
-        def empty_wb(f):
-            for half, src in enumerate((k_ps, v_ps)):
-                empty_rows(wb_g[f][:, 1024 * half : 1024 * (half + 1)], src, "s")
+        def empty_wb(n):
+            f, half = divmod(n, 2)
+            empty_rows(wb_g[f][:, 1024 * half : 1024 * (half + 1)], (k_ps, v_ps)[half], "s")
 
-        for s in range(TILES + 7):
-            run(finish_v, s - 7)
-            run(turn_x, s)
-            run_pair(turn_c, s - 5)
-            if s in (0, 1):
-                prepare_wb(s)
-            run(widen, s + 2)
-            run_pair(rope_products, s - 4)
-            run(normalise, s - 3)
-            run_pair(rope_sum, s - 4)
-            run(empty_x, s)
-            if s in (0, 1):
-                empty_wb(s)
-            run_pair(empty_c, s - 5)
-            run(mm_l, s - 2)
-            run(mm_b, s - 6)
-            run(mm_r, s - 2)
-            run_pair(quant_x, s - 1)
-            run_pair(quant_c, s - 5)
-            if s in (0, 1):
-                quantize(wb_codes[s], wb_sc[s], wb_g[s])
-            run(sum_squares, s - 2)
-            run(finish_k, s - 6)
-            run(inv_root, s - 2)
-            run(store_k, s - 6)
+        nc.scalar.activation(out=warm[0][:], in_=one[:], func=ACT.Sin)
+        for n in range(5):
+            keep_clock()
+        for half in range(2):
+            spread(scale_raw, 4 * half, xt_ps[half])
+            keep_clock()
+        for half in range(2):
+            empty_scale(half, xt_ps[half])
+        for u in range(2):
+            turn_wl(0, u, l_ps[u])
+            keep_clock()
+            empty_wl(0, u, l_ps[u], "s")
+        build_planes()
+        nc.vector.tensor_copy(out=gain_wide[:], in_=gain_raw[:])
+        widen(0)
+        for u, dst in enumerate((k_ps, v_ps)):
+            turn_wl(1, u, dst)
+            keep_clock()
+            empty_wl(1, u, dst, "s")
+        turn_x(0)
+        keep_clock()
+        turn_rows(wr_raw[:], r_ps)
+        keep_clock()
+        spread(gain_wide, 0, l_ps[1])
+        empty_x(0)
+        empty_rows(wr_g[:], r_ps, "s")
+        nc.scalar.activation(out=warm[1][:], in_=one[:], func=ACT.Abs_reciprocal_sqrt)
+        quantize(wl_codes[0], wl_sc[0], wl_g[0])
+        widen(1)
+        build_table(0, "v")
+        quantize(wl_codes[1], wl_sc[1], wl_g[1])
+
+        for s in range(TILES):
+            if s >= 3:
+                mm_b(s - 3, 0, k_ps)
+                mm_b(s - 3, 1, v_ps)
+            if s > 0:
+                run(widen, s + 1)
+            run(rope_sum, s - 2)
+            run(turn_c, s - 2)
+            run(turn_x, s + 1)
+            run(sum_squares, s - 1)
+            if s >= 3:
+                finish_k(s - 3, k_ps)
+                store_k(s - 3)
+            if s in (1, 2):
+                empty_wb(2 * s - 2)
+            run(empty_c, s - 2)
+            run(inv_root, s - 1)
+            if s in (1, 2):
+                empty_wb(2 * s - 1)
+            if 3 <= s < TILES - 1:
+                finish_v(s - 3, v_ps, "s")
+            run(empty_x, s + 1)
+            quant_x(s)
+            if s == 0:
+                empty_gain(l_ps[1])
+                quantize(wr_codes, wr_sc, wr_g)
+                build_table(1, "v")
+            run(quant_c, s - 2)
+            run(rope_products, s - 1)
+            run(normalise, s - 1)
+            if s in (1, 2):
+                quantize(wb_codes[s - 1], wb_sc[s - 1], wb_g[s - 1])
+            mm_l(s)
+            mm_r(s)
+            if s < 2:
+                for half in range(2):
+                    turn_wb(2 * s + half)
+                    keep_clock()
+
+        last = TILES - 1
+        finish_v(last - 3, v_ps, "v")
+        turn_c(last - 1)
+        mm_b(last - 2, 0, k_ps)
+        mm_b(last - 2, 1, v_ps)
+        sum_squares(last)
+        empty_c(last - 1)
+        inv_root(last)
+        rope_sum(last - 1)
+        rope_products(last)
+        quant_c(last - 1)
+        normalise(last)
+        mm_b(last - 1, 0, xt_ps[0])
+        mm_b(last - 1, 1, xt_ps[1])
+        turn_c(last)
+        finish_k(last - 2, k_ps)
+        store_k(last - 2)
+        finish_v(last - 2, v_ps, "s")
+        empty_c(last)
+        rope_sum(last)
+        quant_c(last)
+        mm_b(last, 0, l_ps[0])
+        mm_b(last, 1, l_ps[1])
+        finish_k(last - 1, xt_ps[0])
+        store_k(last - 1)
+        finish_v(last - 1, xt_ps[1], "v")
+        finish_k(last, l_ps[0])
+        store_k(last)
+        finish_v(last, l_ps[1], "v")

@@ -86,25 +86,29 @@ def tile_multiheadlatentattention_pb_t_kernel(tc, x_bytes, x_scale, w_kva, kva_n
         planes = ring("planes", 1, [P, 3, POS_TILES * HALF], F32)[0]
         table = ring("table", 1, [P, POS_TILES, 2, HALF, 2], F32)[0]
         zeros = ring("zeros", 1, [P, 512], BF16)[0]
-        nc.vector.memset(one[:], 1.0)
         nc.vector.memset(zeros[:], 0.0)
+        nc.vector.memset(one[:], 1.0)
 
         def keep_clock():
             nc.tensor.matmul(ct_ps[:], lhsT=zeros[:, 0:P], rhs=zeros[:], start=True, stop=True)
 
         for q in range(8):
-            nc.vector.tensor_scalar(out=coarse[:, q, :], in0=pos[:], scalar1=THETA ** (-8 * q / HALF) / (2 * math.pi), scalar2=None, op0=ALU.mult)
-        for q in range(8):
             nc.vector.tensor_scalar(out=fine[:, q : q + 1], in0=one[:], scalar1=THETA ** (-q / HALF), scalar2=None, op0=ALU.mult)
-        nc.vector.tensor_tensor(
-            out=turns[:],
-            in0=coarse[:].rearrange("p q s -> p s q").unsqueeze(3).to_broadcast([P, POS_TILES, 8, 8]),
-            in1=fine[:].unsqueeze(1).unsqueeze(1).to_broadcast([P, POS_TILES, 8, 8]),
-            op=ALU.mult,
-        )
+        for q in range(8):
+            nc.vector.tensor_scalar(out=coarse[:, q, :], in0=pos[:], scalar1=THETA ** (-8 * q / HALF) / (2 * math.pi), scalar2=None, op0=ALU.mult)
         turns_flat = turns[:].rearrange("p s q r -> p (s q r)")
-        nc.vector.tensor_copy(out=whole[:], in_=turns_flat)
-        nc.vector.tensor_tensor(out=frac[:], in0=turns_flat, in1=whole[:], op=ALU.subtract)
+        halves = [slice(0, 4 * HALF), slice(4 * HALF, 8 * HALF)]
+        for n in range(2):
+            nc.vector.tensor_tensor(
+                out=turns[:, 4 * n : 4 * n + 4, :, :],
+                in0=coarse[:, :, 4 * n : 4 * n + 4].rearrange("p q s -> p s q").unsqueeze(3).to_broadcast([P, 4, 8, 8]),
+                in1=fine[:].unsqueeze(1).unsqueeze(1).to_broadcast([P, 4, 8, 8]),
+                op=ALU.mult,
+            )
+        for cols in halves:
+            nc.vector.tensor_copy(out=whole[:, cols], in_=turns_flat[:, cols])
+        for cols in halves:
+            nc.vector.tensor_tensor(out=frac[:, cols], in0=turns_flat[:, cols], in1=whole[:, cols], op=ALU.subtract)
         warm = ring("warm", 2, [P, 1], F32)
 
         def build_planes():
@@ -124,8 +128,8 @@ def tile_multiheadlatentattention_pb_t_kernel(tc, x_bytes, x_scale, w_kva, kva_n
             for j in range(4):
                 nc.tensor.transpose(dst[:, P * j : P * (j + 1)], src[:, first + j : first + j + 1].to_broadcast([P, P]), ident[:])
 
-        def empty_scale(half, src):
-            nc.scalar.copy(out=scale[:].rearrange("p (n j) -> p n j", j=8)[:, :, 4 * half : 4 * half + 4], in_=src[:].rearrange("p (j n) -> p n j", j=4))
+        def empty_scale(half, src, engine):
+            copy_on(engine, scale[:].rearrange("p (n j) -> p n j", j=8)[:, :, 4 * half : 4 * half + 4], src[:].rearrange("p (j n) -> p n j", j=4))
 
         def empty_gain(src):
             nc.vector.tensor_copy(out=gain[:].rearrange("p (u m e) -> p u m e", u=2, e=2), in_=src[:].rearrange("p (u e m) -> p u m e", u=2, e=2))
@@ -283,8 +287,8 @@ def tile_multiheadlatentattention_pb_t_kernel(tc, x_bytes, x_scale, w_kva, kva_n
         for half in range(2):
             spread(scale_raw, 4 * half, xt_ps[half])
             keep_clock()
-        for half in range(2):
-            empty_scale(half, xt_ps[half])
+        empty_scale(0, xt_ps[0], "s")
+        empty_scale(1, xt_ps[1], "s")
         for u in range(2):
             turn_wl(0, u, l_ps[u])
             keep_clock()
@@ -308,72 +312,70 @@ def tile_multiheadlatentattention_pb_t_kernel(tc, x_bytes, x_scale, w_kva, kva_n
         widen(1)
         build_table(0, "v")
         quantize(wl_codes[1], wl_sc[1], wl_g[1])
+        quant_x(0)
+        empty_gain(l_ps[1])
+        quantize(wr_codes, wr_sc, wr_g)
+        build_table(1, "v")
 
-        for s in range(TILES):
-            if s >= 3:
-                mm_b(s - 3, 0, k_ps)
-                mm_b(s - 3, 1, v_ps)
-            if s > 0:
-                run(widen, s + 1)
+        widen(2)
+
+        for s in range(1, TILES + 1):
+            if s >= 5:
+                finish_v(s - 5, v_ps, "s" if s + 2 < TILES else "v")
+            run(turn_x, s)
+            run(turn_c, s - 3)
+            run(widen, s + 2)
+            if s == 4:
+                quantize(wb_codes[1], wb_sc[1], wb_g[1])
+            run(rope_products, s - 2)
+            run(normalise, s - 2)
             run(rope_sum, s - 2)
-            run(turn_c, s - 2)
-            run(turn_x, s + 1)
-            run(sum_squares, s - 1)
-            if s >= 3:
-                finish_k(s - 3, k_ps)
-                store_k(s - 3)
-            if s in (1, 2):
-                empty_wb(2 * s - 2)
-            run(empty_c, s - 2)
-            run(inv_root, s - 1)
-            if s in (1, 2):
-                empty_wb(2 * s - 1)
-            if 3 <= s < TILES - 1:
-                finish_v(s - 3, v_ps, "s")
-            run(empty_x, s + 1)
-            quant_x(s)
-            if s == 0:
-                empty_gain(l_ps[1])
-                quantize(wr_codes, wr_sc, wr_g)
-                build_table(1, "v")
-            run(quant_c, s - 2)
-            run(rope_products, s - 1)
-            run(normalise, s - 1)
-            if s in (1, 2):
-                quantize(wb_codes[s - 1], wb_sc[s - 1], wb_g[s - 1])
-            mm_l(s)
-            mm_r(s)
-            if s < 2:
-                for half in range(2):
-                    turn_wb(2 * s + half)
-                    keep_clock()
+            run(empty_x, s)
+            run(empty_c, s - 3)
+            mm_l(s - 1)
+            if s >= 4:
+                mm_b(s - 4, 0, k_ps)
+                mm_b(s - 4, 1, v_ps)
+            mm_r(s - 1)
+            if s in (1, 2, 3):
+                for n in ((0, 1), (2,), (3,))[s - 1]:
+                    turn_wb(n)
+            run(quant_x, s)
+            run(quant_c, s - 3)
+            if s == 2:
+                quantize(wb_codes[0], wb_sc[0], wb_g[0])
+            sum_squares(s - 1)
+            if s >= 4:
+                finish_k(s - 4, k_ps)
+                store_k(s - 4)
+            inv_root(s - 1)
+            if s in (1, 2, 3):
+                for n in ((0, 1), (2,), (3,))[s - 1]:
+                    empty_wb(n)
 
         last = TILES - 1
-        finish_v(last - 3, v_ps, "v")
         turn_c(last - 1)
-        mm_b(last - 2, 0, k_ps)
-        mm_b(last - 2, 1, v_ps)
-        sum_squares(last)
+        mm_b(last - 2, 0, xt_ps[0])
+        mm_b(last - 2, 1, xt_ps[1])
+        finish_v(last - 3, v_ps, "v")
+        normalise(last)
         empty_c(last - 1)
-        inv_root(last)
-        rope_sum(last - 1)
+        turn_c(last)
         rope_products(last)
         quant_c(last - 1)
-        normalise(last)
-        mm_b(last - 1, 0, xt_ps[0])
-        mm_b(last - 1, 1, xt_ps[1])
-        turn_c(last)
-        finish_k(last - 2, k_ps)
+        finish_k(last - 2, xt_ps[0])
         store_k(last - 2)
-        finish_v(last - 2, v_ps, "s")
         empty_c(last)
+        mm_b(last - 1, 0, k_ps)
+        mm_b(last - 1, 1, v_ps)
         rope_sum(last)
+        finish_v(last - 2, xt_ps[1], "v")
         quant_c(last)
         mm_b(last, 0, l_ps[0])
         mm_b(last, 1, l_ps[1])
-        finish_k(last - 1, xt_ps[0])
+        finish_k(last - 1, k_ps)
         store_k(last - 1)
-        finish_v(last - 1, xt_ps[1], "v")
+        finish_v(last - 1, v_ps, "v")
         finish_k(last, l_ps[0])
         store_k(last)
         finish_v(last, l_ps[1], "v")

@@ -25,6 +25,7 @@ GROUPS = B * T // (P * ROWS)
 TILES = GROUPS * ROWS
 POS_TILES = T // P
 HALF = R // 2
+WHOLE_FROM = 30
 
 
 def tile_multiheadlatentattention_pb_t_kernel(tc, x_bytes, x_scale, w_kva, kva_norm_w, w_kvb, out_0, out_1):
@@ -132,7 +133,7 @@ def tile_multiheadlatentattention_pb_t_kernel(tc, x_bytes, x_scale, w_kva, kva_n
             copy_on(engine, scale[:].rearrange("p (n j) -> p n j", j=8)[:, :, 4 * half : 4 * half + 4], src[:].rearrange("p (j n) -> p n j", j=4))
 
         def empty_gain(src):
-            nc.vector.tensor_copy(out=gain[:].rearrange("p (u m e) -> p u m e", u=2, e=2), in_=src[:].rearrange("p (u e m) -> p u m e", u=2, e=2))
+            nc.scalar.copy(out=gain[:].rearrange("p (u m e) -> p u m e", u=2, e=2), in_=src[:].rearrange("p (u e m) -> p u m e", u=2, e=2))
 
         wl_g = ring("wl_g", 2, [P, 2048], BF16)
         wl_codes = ring("wl_codes", 2, [P, 512], U32)
@@ -188,6 +189,7 @@ def tile_multiheadlatentattention_pb_t_kernel(tc, x_bytes, x_scale, w_kva, kva_n
         prod = ring("prod", 2, [P, 2 * R], F32)
         rope = ring("rope", 6, [P, 1, R], F32)
         kout = ring("kout", 6, [P, H, R], F32)
+        krow = ring("krow", TILES - WHOLE_FROM, [P, H, 2 * R], F32)
         vout = ring("vout", 6, [P, H * VD], F32)
 
         def at(tiles, i):
@@ -238,8 +240,14 @@ def tile_multiheadlatentattention_pb_t_kernel(tc, x_bytes, x_scale, w_kva, kva_n
             )
 
         def rope_sum(i):
-            nc.vector.tensor_tensor(out=at(rope, i)[:, 0, :], in0=at(prod, i)[:, 0:R], in1=at(prod, i)[:, R : 2 * R], op=ALU.add)
-            nc.sync.dma_start(out=k_hbm[i // ROWS, i % ROWS][:, :, R : 2 * R], in_=at(rope, i)[:].to_broadcast([P, H, R]))
+            out = at(rope, i)[:, 0, :] if i < WHOLE_FROM else at(krow, i)[:, 0, R : 2 * R]
+            nc.vector.tensor_tensor(out=out, in0=at(prod, i)[:, 0:R], in1=at(prod, i)[:, R : 2 * R], op=ALU.add)
+            if i < WHOLE_FROM:
+                nc.sync.dma_start(out=k_hbm[i // ROWS, i % ROWS][:, :, R : 2 * R], in_=at(rope, i)[:].to_broadcast([P, H, R]))
+
+        def rope_spread(i):
+            if i >= WHOLE_FROM:
+                nc.vector.tensor_copy(out=at(krow, i)[:, 1:H, R : 2 * R], in_=at(krow, i)[:, 0:1, R : 2 * R].to_broadcast([P, H - 1, R]))
 
         def turn_c(i):
             words = at(cn, i)[:].bitcast(F32)
@@ -259,10 +267,14 @@ def tile_multiheadlatentattention_pb_t_kernel(tc, x_bytes, x_scale, w_kva, kva_n
             )
 
         def finish_k(i, src):
-            nc.scalar.copy(out=at(kout, i)[:].rearrange("p h d -> p (h d)"), in_=src[:])
+            out = at(kout, i)[:] if i < WHOLE_FROM else at(krow, i)[:, :, 0:R]
+            nc.scalar.copy(out=out, in_=src[:].rearrange("p (h d) -> p h d", h=H))
 
         def store_k(i):
-            nc.sync.dma_start(out=k_hbm[i // ROWS, i % ROWS][:, :, 0:R], in_=at(kout, i)[:])
+            if i < WHOLE_FROM:
+                nc.sync.dma_start(out=k_hbm[i // ROWS, i % ROWS][:, :, 0:R], in_=at(kout, i)[:])
+            else:
+                nc.sync.dma_start(out=k_hbm[i // ROWS, i % ROWS], in_=at(krow, i)[:])
 
         def finish_v(i, src, engine):
             copy_on(engine, at(vout, i)[:], src[:])
@@ -313,7 +325,6 @@ def tile_multiheadlatentattention_pb_t_kernel(tc, x_bytes, x_scale, w_kva, kva_n
         build_table(0, "v")
         quantize(wl_codes[1], wl_sc[1], wl_g[1])
         quant_x(0)
-        empty_gain(l_ps[1])
         quantize(wr_codes, wr_sc, wr_g)
         build_table(1, "v")
 
@@ -324,13 +335,15 @@ def tile_multiheadlatentattention_pb_t_kernel(tc, x_bytes, x_scale, w_kva, kva_n
                 finish_v(s - 5, v_ps, "s" if s + 2 < TILES else "v")
             run(turn_x, s)
             run(turn_c, s - 3)
-            run(widen, s + 2)
+            run(rope_products, s - 2)
             if s == 4:
                 quantize(wb_codes[1], wb_sc[1], wb_g[1])
-            run(rope_products, s - 2)
+            run(widen, s + 2)
             run(normalise, s - 2)
             run(rope_sum, s - 2)
             run(empty_x, s)
+            if s == 1:
+                empty_gain(l_ps[1])
             run(empty_c, s - 3)
             mm_l(s - 1)
             if s >= 4:
@@ -341,6 +354,7 @@ def tile_multiheadlatentattention_pb_t_kernel(tc, x_bytes, x_scale, w_kva, kva_n
                 for n in ((0, 1), (2,), (3,))[s - 1]:
                     turn_wb(n)
             run(quant_x, s)
+            run(rope_spread, s - 2)
             run(quant_c, s - 3)
             if s == 2:
                 quantize(wb_codes[0], wb_sc[0], wb_g[0])
@@ -371,6 +385,7 @@ def tile_multiheadlatentattention_pb_t_kernel(tc, x_bytes, x_scale, w_kva, kva_n
         rope_sum(last)
         finish_v(last - 2, xt_ps[1], "v")
         quant_c(last)
+        rope_spread(last)
         mm_b(last, 0, l_ps[0])
         mm_b(last, 1, l_ps[1])
         finish_k(last - 1, k_ps)

@@ -86,12 +86,7 @@ def tile_multiheadlatentattention_pb_t_kernel(tc, x_bytes, x_scale, w_kva, kva_n
         mag = ring("mag", 1, [P, POS_TILES * HALF], F32)[0]
         planes = ring("planes", 1, [P, 3, POS_TILES * HALF], F32)[0]
         table = ring("table", 1, [P, POS_TILES, 2, HALF, 2], F32)[0]
-        zeros = ring("zeros", 1, [P, 512], BF16)[0]
-        nc.vector.memset(zeros[:], 0.0)
         nc.vector.memset(one[:], 1.0)
-
-        def keep_clock():
-            nc.tensor.matmul(ct_ps[:], lhsT=zeros[:, 0:P], rhs=zeros[:], start=True, stop=True)
 
         for q in range(8):
             nc.vector.tensor_scalar(out=fine[:, q : q + 1], in0=one[:], scalar1=THETA ** (-q / HALF), scalar2=None, op0=ALU.mult)
@@ -110,12 +105,11 @@ def tile_multiheadlatentattention_pb_t_kernel(tc, x_bytes, x_scale, w_kva, kva_n
             nc.vector.tensor_copy(out=whole[:, cols], in_=turns_flat[:, cols])
         for cols in halves:
             nc.vector.tensor_tensor(out=frac[:, cols], in0=turns_flat[:, cols], in1=whole[:, cols], op=ALU.subtract)
-        warm = ring("warm", 2, [P, 1], F32)
 
         def build_planes():
-            nc.scalar.activation(out=mag[:], in_=frac[:], func=ACT.Abs)
             nc.scalar.activation(out=planes[:, 0, :], in_=frac[:], func=ACT.Sin, scale=-2 * math.pi)
             nc.scalar.activation(out=planes[:, 2, :], in_=frac[:], func=ACT.Sin, scale=2 * math.pi)
+            nc.scalar.activation(out=mag[:], in_=frac[:], func=ACT.Abs)
             nc.scalar.activation(out=planes[:, 1, :], in_=mag[:], func=ACT.Sin, scale=-2 * math.pi, bias=math.pi / 2)
 
         def build_table(a, engine):
@@ -293,33 +287,24 @@ def tile_multiheadlatentattention_pb_t_kernel(tc, x_bytes, x_scale, w_kva, kva_n
             f, half = divmod(n, 2)
             empty_rows(wb_g[f][:, 1024 * half : 1024 * (half + 1)], (k_ps, v_ps)[half], "s")
 
-        nc.scalar.activation(out=warm[0][:], in_=one[:], func=ACT.Sin)
-        for n in range(5):
-            keep_clock()
         for half in range(2):
             spread(scale_raw, 4 * half, xt_ps[half])
-            keep_clock()
-        empty_scale(0, xt_ps[0], "s")
-        empty_scale(1, xt_ps[1], "s")
+        build_planes()
+        empty_scale(0, xt_ps[0], "v")
+        empty_scale(1, xt_ps[1], "v")
         for u in range(2):
             turn_wl(0, u, l_ps[u])
-            keep_clock()
-            empty_wl(0, u, l_ps[u], "s")
-        build_planes()
+            empty_wl(0, u, l_ps[u], "v")
         nc.vector.tensor_copy(out=gain_wide[:], in_=gain_raw[:])
         widen(0)
         for u, dst in enumerate((k_ps, v_ps)):
             turn_wl(1, u, dst)
-            keep_clock()
             empty_wl(1, u, dst, "s")
         turn_x(0)
-        keep_clock()
         turn_rows(wr_raw[:], r_ps)
-        keep_clock()
         spread(gain_wide, 0, l_ps[1])
         empty_x(0)
         empty_rows(wr_g[:], r_ps, "s")
-        nc.scalar.activation(out=warm[1][:], in_=one[:], func=ACT.Abs_reciprocal_sqrt)
         quantize(wl_codes[0], wl_sc[0], wl_g[0])
         widen(1)
         build_table(0, "v")

import math
from contextlib import ExitStack

import concourse.mybir as mybir
from concourse.masks import make_identity

B, T, C, H, R, KVL, VD = 4, 1024, 1024, 4, 128, 512, 128
THETA = 10000.0
EPS = 1e-6
FLOPS = 2 * B * T * C * (KVL + R) + 2 * B * T * KVL * H * (R + VD)

F32 = mybir.dt.float32
BF16 = mybir.dt.bfloat16
I32 = mybir.dt.int32
U32 = mybir.dt.uint32
U8 = mybir.dt.uint8
FP8 = mybir.dt.float8_e4m3fn
FP8X4 = mybir.dt.float8_e4m3fn_x4
ALU = mybir.AluOpType
ACT = mybir.ActivationFunctionType

P = 128
ROWS = 4
GROUPS = B * T // (P * ROWS)
TILES = GROUPS * ROWS
POS_TILES = T // P
HALF = R // 2
WHOLE_FROM = 30


def tile_multiheadlatentattention_pb_t_kernel(tc, x_bytes, x_scale, w_kva, kva_norm_w, w_kvb, out_0, out_1):
    nc = tc.nc
    with ExitStack() as ctx:
        sb = ctx.enter_context(tc.tile_pool(name="sb", bufs=1))
        ps = ctx.enter_context(tc.psum_pool(name="ps", bufs=1))
        ctx.enter_context(tc.manual_schedule())

        def ring(name, count, shape, dtype):
            return [sb.tile(shape, dtype, name="%s%d" % (name, n), align_bytes=64) for n in range(count)]

        def bank(name):
            return ps.tile([P, 512], F32, name=name)

        xt_ps = [bank("xt0"), bank("xt1")]
        l_ps = [bank("l0"), bank("l1")]
        r_ps = bank("rp")
        ct_ps = bank("ct")
        k_ps = bank("kp")
        v_ps = bank("vp")

        wl_raw = ring("wl_raw", 2, [P, 4, 512], BF16)
        wr_raw = ring("wr_raw", 1, [P, C], BF16)[0]
        wb_raw = ring("wb_raw", 2, [P, H, KVL], BF16)
        scale = ring("scale", 1, [P, C], F32)[0]
        scale_raw = ring("scale_raw", 1, [P, C // P], F32)[0]
        gain_raw = ring("gain_raw", 1, [P, KVL // P], BF16)[0]
        xbytes = ring("xbytes", GROUPS, [P, ROWS * C], U8)
        wl_hbm = w_kva[0:KVL, :].rearrange("(m t) k -> m t k", t=4)
        wb_hbm = w_kvb.rearrange("(h f d) k -> f d h k", f=2, d=P)
        x_hbm = x_bytes.rearrange("b (s p j) k -> (b s) p (j k)", p=P, j=ROWS)
        k_hbm = out_0.rearrange("b (s p j) h d -> (b s) j p h d", p=P, j=ROWS)
        v_hbm = out_1.rearrange("b (s p j) h d -> (b s) j p (h d)", p=P, j=ROWS)

        nc.sync.dma_start(out=scale_raw[:], in_=x_scale.rearrange("a o (p j) -> p (a o j)", p=P))
        nc.sync.dma_start(out=gain_raw[:], in_=kva_norm_w.rearrange("(p j) -> p j", p=P))
        nc.sync.dma_start(out=wl_raw[0][:], in_=wl_hbm[:, :, 0:512])
        nc.sync.dma_start(out=xbytes[0][:], in_=x_hbm[0])
        nc.sync.dma_start(out=wl_raw[1][:], in_=wl_hbm[:, :, 512:1024])
        nc.sync.dma_start(out=wr_raw[:], in_=w_kva[KVL : KVL + R, :])
        for f in range(2):
            nc.sync.dma_start(out=wb_raw[f][:], in_=wb_hbm[f])
        for n in range(1, GROUPS):
            nc.sync.dma_start(out=xbytes[n][:], in_=x_hbm[n])

        pos = ring("pos", 1, [P, POS_TILES], I32)[0]
        nc.gpsimd.iota(pos[:], pattern=[[P * ROWS, POS_TILES // ROWS], [1, ROWS]], base=0, channel_multiplier=ROWS)
        ident = ring("ident", 1, [P, P], F32)[0]
        make_identity(nc, ident[:])

        fine = ring("fine", 1, [P, 8], F32)[0]
        one = ring("one", 1, [P, 1], F32)[0]
        coarse = ring("coarse", 1, [P, 8, POS_TILES], F32)[0]
        turns = ring("turns", 1, [P, POS_TILES, 8, 8], F32)[0]
        whole = ring("whole", 1, [P, POS_TILES * HALF], I32)[0]
        frac = ring("frac", 1, [P, POS_TILES * HALF], F32)[0]
        mag = ring("mag", 1, [P, POS_TILES * HALF], F32)[0]
        planes = ring("planes", 1, [P, 3, POS_TILES * HALF], F32)[0]
        table = ring("table", 1, [P, POS_TILES, 2, HALF, 2], F32)[0]
        nc.vector.memset(one[:], 1.0)

        for q in range(8):
            nc.vector.tensor_scalar(out=fine[:, q : q + 1], in0=one[:], scalar1=THETA ** (-q / HALF), scalar2=None, op0=ALU.mult)
        for q in range(8):
            nc.vector.tensor_scalar(out=coarse[:, q, :], in0=pos[:], scalar1=THETA ** (-8 * q / HALF) / (2 * math.pi), scalar2=None, op0=ALU.mult)
        turns_flat = turns[:].rearrange("p s q r -> p (s q r)")
        halves = [slice(0, 4 * HALF), slice(4 * HALF, 8 * HALF)]
        for n in range(2):
            nc.vector.tensor_tensor(
                out=turns[:, 4 * n : 4 * n + 4, :, :],
                in0=coarse[:, :, 4 * n : 4 * n + 4].rearrange("p q s -> p s q").unsqueeze(3).to_broadcast([P, 4, 8, 8]),
                in1=fine[:].unsqueeze(1).unsqueeze(1).to_broadcast([P, 4, 8, 8]),
                op=ALU.mult,
            )
        for cols in halves:
            nc.vector.tensor_copy(out=whole[:, cols], in_=turns_flat[:, cols])
        for cols in halves:
            nc.vector.tensor_tensor(out=frac[:, cols], in0=turns_flat[:, cols], in1=whole[:, cols], op=ALU.subtract)

        def build_planes():
            nc.scalar.activation(out=planes[:, 0, :], in_=frac[:], func=ACT.Sin, scale=-2 * math.pi)
            nc.scalar.activation(out=planes[:, 2, :], in_=frac[:], func=ACT.Sin, scale=2 * math.pi)
            nc.scalar.activation(out=mag[:], in_=frac[:], func=ACT.Abs)
            nc.scalar.activation(out=planes[:, 1, :], in_=mag[:], func=ACT.Sin, scale=-2 * math.pi, bias=math.pi / 2)

        def build_table(a, engine):
            copy_on(engine, table[:, :, a, :, :], planes[:, 1 - a : 3 - a, :].rearrange("p b (s j) -> p s j b", j=HALF))

        gain = ring("gain", 1, [P, KVL], F32)[0]

        gain_wide = ring("gain_wide", 1, [P, KVL // P], F32)[0]

        def spread(src, first, dst):
            for j in range(4):
                nc.tensor.transpose(dst[:, P * j : P * (j + 1)], src[:, first + j : first + j + 1].to_broadcast([P, P]), ident[:])

        def empty_scale(half, src, engine):
            copy_on(engine, scale[:].rearrange("p (n j) -> p n j", j=8)[:, :, 4 * half : 4 * half + 4], src[:].rearrange("p (j n) -> p n j", j=4))

        def empty_gain(src):
            nc.scalar.copy(out=gain[:].rearrange("p (u m e) -> p u m e", u=2, e=2), in_=src[:].rearrange("p (u e m) -> p u m e", u=2, e=2))

        wl_g = ring("wl_g", 2, [P, 2048], BF16)
        wl_codes = ring("wl_codes", 2, [P, 512], U32)
        wl_sc = ring("wl_sc", 2, [P, 512], U8)
        wr_g = ring("wr_g", 1, [P, 1024], BF16)[0]
        wr_codes = ring("wr_codes", 1, [P, 256], U32)[0]
        wr_sc = ring("wr_sc", 1, [P, 256], U8)[0]
        wb_g = ring("wb_g", 2, [P, 2048], BF16)
        wb_codes = ring("wb_codes", 2, [P, 512], U32)
        wb_sc = ring("wb_sc", 2, [P, 512], U8)

        def copy_on(engine, out, in_):
            if engine == "v":
                nc.vector.tensor_copy(out=out, in_=in_)
            else:
                nc.scalar.copy(out=out, in_=in_)

        def quantize(codes, sc, src):
            nc.vector.quantize_mx(out=codes[:].bitcast(FP8X4), scales=sc[:], in_=src[:])

        def turn_pass(dst, col, words, start):
            for w in range(2):
                nc.tensor.transpose(dst[:, col + P * w : col + P * (w + 1)], words[:, start + w : start + 256 : 2], ident[:])

        def turn_wl(g, u, dst):
            words = wl_raw[g][:].rearrange("p t k -> p (t k)").bitcast(F32)
            for e in range(2):
                turn_pass(dst, 256 * e, words, 256 * (2 * u + e))

        def empty_wl(g, u, src, engine):
            out = wl_g[g][:].bitcast(F32)[:, 512 * u : 512 * (u + 1)].rearrange("p (m n) -> p m n", n=4)
            copy_on(engine, out, src[:].rearrange("p (n m) -> p m n", n=4))

        def turn_rows(raw, dst):
            words = raw.bitcast(F32)
            for g in range(2):
                turn_pass(dst, 256 * g, words, 256 * g)

        def empty_rows(out, src, engine):
            copy_on(engine, out.bitcast(F32).rearrange("p (g r w) -> p g r w", g=2, w=2), src[:].rearrange("p (g w r) -> p g r w", g=2, w=2))

        xw = ring("xw", 4, [P, C], BF16)
        xg = ring("xg", 2, [P, C], BF16)
        x_codes = ring("x_codes", 3, [P, 256], U32)
        x_sc = ring("x_sc", 3, [P, 256], U8)
        squares = ring("squares", 2, [P, KVL], BF16)
        ssum = ring("ssum", 3, [P, 1], F32)
        rstd = ring("rstd", 3, [P, 1], F32)
        cn = ring("cn", 3, [P, KVL], BF16)
        cg = ring("cg", 2, [P, KVL], BF16)
        c_codes = ring("c_codes", 3, [P, P], U32)
        c_sc = ring("c_sc", 3, [P, P], U8)
        prod = ring("prod", 2, [P, 2 * R], F32)
        rope = ring("rope", 6, [P, 1, R], F32)
        kout = ring("kout", 6, [P, H, R], F32)
        krow = ring("krow", TILES - WHOLE_FROM, [P, H, 2 * R], F32)
        vout = ring("vout", 6, [P, H * VD], F32)

        def at(tiles, i):
            return tiles[i % len(tiles)]

        def widen(i):
            src = xbytes[i // ROWS][:, C * (i % ROWS) : C * (i % ROWS + 1)]
            nc.vector.tensor_tensor(out=at(xw, i)[:], in0=src.bitcast(FP8), in1=scale[:], op=ALU.mult)

        def turn_x(i):
            turn_rows(at(xw, i)[:], at(xt_ps, i))

        def empty_x(i):
            empty_rows(at(xg, i)[:], at(xt_ps, i), "s")

        def quant_x(i):
            quantize(at(x_codes, i), at(x_sc, i), at(xg, i))

        def mm_a(i, out, codes, sc):
            for g in range(2):
                cols = slice(P * g, P * (g + 1))
                nc.tensor.matmul_mx(
                    out=out, lhsT=at(x_codes, i)[:, cols].bitcast(FP8X4), lhsT_scale=at(x_sc, i)[:, cols],
                    rhs=codes[g].bitcast(FP8X4), rhs_scale=sc[g], start=(g == 0), stop=(g == 1),
                )

        def mm_l(i):
            mm_a(i, at(l_ps, i)[:], [t[:] for t in wl_codes], [t[:] for t in wl_sc])

        def mm_r(i):
            mm_a(i, r_ps[:, 0:R], [wr_codes[:, 0:P], wr_codes[:, P : 2 * P]], [wr_sc[:, 0:P], wr_sc[:, P : 2 * P]])

        def sum_squares(i):
            nc.scalar.activation(out=at(squares, i)[:], in_=at(l_ps, i)[:], func=ACT.Square, accum_out=at(ssum, i)[:])

        def inv_root(i):
            nc.scalar.activation(out=at(rstd, i)[:], in_=at(ssum, i)[:], func=ACT.Abs_reciprocal_sqrt, scale=1.0 / KVL, bias=EPS)

        def normalise(i):
            nc.vector.scalar_tensor_tensor(out=at(cn, i)[:], in0=at(l_ps, i)[:], scalar=at(rstd, i)[:], in1=gain[:], op0=ALU.mult, op1=ALU.mult)

        def rope_products(i):
            nc.vector.tensor_tensor(
                out=at(prod, i)[:].rearrange("p (a j b) -> p a j b", a=2, b=2),
                in0=r_ps[:, 0:R].rearrange("p (j a) -> p a j", a=2).unsqueeze(3).to_broadcast([P, 2, HALF, 2]),
                in1=table[:, i % POS_TILES, :, :, :],
                op=ALU.mult,
            )

        def rope_sum(i):
            out = at(rope, i)[:, 0, :] if i < WHOLE_FROM else at(krow, i)[:, 0, R : 2 * R]
            nc.vector.tensor_tensor(out=out, in0=at(prod, i)[:, 0:R], in1=at(prod, i)[:, R : 2 * R], op=ALU.add)
            if i < WHOLE_FROM:
                nc.sync.dma_start(out=k_hbm[i // ROWS, i % ROWS][:, :, R : 2 * R], in_=at(rope, i)[:].to_broadcast([P, H, R]))

        def rope_spread(i):
            if i >= WHOLE_FROM:
                nc.vector.tensor_copy(out=at(krow, i)[:, 1:H, R : 2 * R], in_=at(krow, i)[:, 0:1, R : 2 * R].to_broadcast([P, H - 1, R]))

        def turn_c(i):
            words = at(cn, i)[:].bitcast(F32)
            for u in range(2):
                nc.tensor.transpose(ct_ps[:, P * u : P * (u + 1)], words[:, P * u : P * (u + 1)], ident[:])

        def empty_c(i):
            nc.scalar.copy(out=at(cg, i)[:].bitcast(F32).rearrange("p (r u) -> p r u", u=2), in_=ct_ps[:, 0 : 2 * P].rearrange("p (u r) -> p r u", u=2))

        def quant_c(i):
            quantize(at(c_codes, i), at(c_sc, i), at(cg, i))

        def mm_b(i, f, out):
            nc.tensor.matmul_mx(
                out=out[:], lhsT=at(c_codes, i)[:].bitcast(FP8X4), lhsT_scale=at(c_sc, i)[:],
                rhs=wb_codes[f][:].bitcast(FP8X4), rhs_scale=wb_sc[f][:], start=True, stop=True,
            )

        def finish_k(i, src):
            out = at(kout, i)[:] if i < WHOLE_FROM else at(krow, i)[:, :, 0:R]
            nc.scalar.copy(out=out, in_=src[:].rearrange("p (h d) -> p h d", h=H))

        def store_k(i):
            if i < WHOLE_FROM:
                nc.sync.dma_start(out=k_hbm[i // ROWS, i % ROWS][:, :, 0:R], in_=at(kout, i)[:])
            else:
                nc.sync.dma_start(out=k_hbm[i // ROWS, i % ROWS], in_=at(krow, i)[:])

        def finish_v(i, src, engine):
            copy_on(engine, at(vout, i)[:], src[:])
            nc.sync.dma_start(out=v_hbm[i // ROWS, i % ROWS], in_=at(vout, i)[:])

        def run(stage, i):
            if 0 <= i < TILES:
                stage(i)

        def turn_wb(n):
            f, half = divmod(n, 2)
            flat = wb_raw[f][:].rearrange("p h k -> p (h k)")
            turn_rows(flat[:, 1024 * half : 1024 * (half + 1)], (k_ps, v_ps)[half])

        def empty_wb(n):
            f, half = divmod(n, 2)
            empty_rows(wb_g[f][:, 1024 * half : 1024 * (half + 1)], (k_ps, v_ps)[half], "s")

        for half in range(2):
            spread(scale_raw, 4 * half, xt_ps[half])
        build_planes()
        empty_scale(0, xt_ps[0], "v")
        empty_scale(1, xt_ps[1], "v")
        for u in range(2):
            turn_wl(0, u, l_ps[u])
            empty_wl(0, u, l_ps[u], "v")
        nc.vector.tensor_copy(out=gain_wide[:], in_=gain_raw[:])
        widen(0)
        for u, dst in enumerate((k_ps, v_ps)):
            turn_wl(1, u, dst)
            empty_wl(1, u, dst, "s")
        turn_x(0)
        turn_rows(wr_raw[:], r_ps)
        spread(gain_wide, 0, l_ps[1])
        empty_x(0)
        empty_rows(wr_g[:], r_ps, "s")
        quantize(wl_codes[0], wl_sc[0], wl_g[0])
        widen(1)
        build_table(0, "v")
        quantize(wl_codes[1], wl_sc[1], wl_g[1])
        quant_x(0)
        quantize(wr_codes, wr_sc, wr_g)
        build_table(1, "v")

        widen(2)

        for s in range(1, TILES + 1):
            if s >= 5:
                finish_v(s - 5, v_ps, "s" if s + 2 < TILES else "v")
            run(turn_x, s)
            run(turn_c, s - 3)
            run(rope_products, s - 2)
            if s == 4:
                quantize(wb_codes[1], wb_sc[1], wb_g[1])
            run(widen, s + 2)
            run(normalise, s - 2)
            run(rope_sum, s - 2)
            run(empty_x, s)
            if s == 1:
                empty_gain(l_ps[1])
            run(empty_c, s - 3)
            mm_l(s - 1)
            if s >= 4:
                mm_b(s - 4, 0, k_ps)
                mm_b(s - 4, 1, v_ps)
            mm_r(s - 1)
            if s in (1, 2, 3):
                for n in ((0, 1), (2,), (3,))[s - 1]:
                    turn_wb(n)
            run(quant_x, s)
            run(rope_spread, s - 2)
            run(quant_c, s - 3)
            if s == 2:
                quantize(wb_codes[0], wb_sc[0], wb_g[0])
            sum_squares(s - 1)
            if s >= 4:
                finish_k(s - 4, k_ps)
                store_k(s - 4)
            inv_root(s - 1)
            if s in (1, 2, 3):
                for n in ((0, 1), (2,), (3,))[s - 1]:
                    empty_wb(n)

        last = TILES - 1
        turn_c(last - 1)
        mm_b(last - 2, 0, xt_ps[0])
        mm_b(last - 2, 1, xt_ps[1])
        finish_v(last - 3, v_ps, "v")
        normalise(last)
        empty_c(last - 1)
        turn_c(last)
        rope_products(last)
        quant_c(last - 1)
        finish_k(last - 2, xt_ps[0])
        store_k(last - 2)
        empty_c(last)
        mm_b(last - 1, 0, k_ps)
        mm_b(last - 1, 1, v_ps)
        rope_sum(last)
        finish_v(last - 2, xt_ps[1], "v")
        quant_c(last)
        rope_spread(last)
        mm_b(last, 0, l_ps[0])
        mm_b(last, 1, l_ps[1])
        finish_k(last - 1, k_ps)
        store_k(last - 1)
        finish_v(last - 1, v_ps, "v")
        finish_k(last, l_ps[0])
        store_k(last)
        finish_v(last, l_ps[1], "v")
